import numpy as np
import ml_dtypes


def mxq(x, axis, fmt="e4m3"):
    dtype, down = {"e4m3": (ml_dtypes.float8_e4m3fn, 7), "e5m2": (ml_dtypes.float8_e5m2, 14)}[fmt]
    v = np.moveaxis(np.asarray(x, np.float32).astype(ml_dtypes.bfloat16).astype(np.float64), axis, -1)
    blocks = v.reshape(v.shape[:-1] + (-1, 32))
    amax = np.abs(blocks).max(-1, keepdims=True)
    byte = np.maximum(np.where(amax > 0, np.frexp(amax)[1] - 1 + 127, 0) - down, 1)
    scale = np.exp2(byte - 127.0)
    codes = (blocks / scale).astype(np.float32).astype(dtype).astype(np.float64)
    return np.moveaxis((codes * scale).reshape(v.shape), -1, axis)


WIDE = False


def mx_kscale(k):
    if not WIDE:
        return np.ones(k)
    levels = np.array([10, -10, 5, -5, 0])
    a = np.random.permutation(np.resize(levels, k // 512 * 4)).reshape(k // 512, 4)
    idx = np.arange(k)
    return np.exp2(a[idx // 512, idx % 128 // 32])


BF16 = ml_dtypes.bfloat16


def bf(x):
    return np.asarray(x, np.float32).astype(BF16)


def f64(x):
    return np.asarray(x).astype(np.float64)


E2M1 = np.array([0.0, 0.5, 1.0, 1.5, 2.0, 3.0, 4.0, 6.0, -0.0, -0.5, -1.0, -1.5, -2.0, -3.0, -4.0, -6.0])


def pack_weight(w, fmt):
    k, n = w.shape
    w = f64(bf(w)).reshape(k // 32, 32, n)
    amax = np.abs(w).max(1)
    if fmt == "e4m3":
        byte = np.frexp(amax)[1] - 1 + 127 - 7
    else:
        mant, ex = np.frexp(amax / 6.0)
        byte = np.where(mant > 0.5, ex, ex - 1) + 127
    byte = np.clip(np.where(amax > 0, byte, 1), 1, 254)
    scaled = (w * np.exp2(127.0 - byte)[:, None, :]).reshape(k, n).astype(np.float32)
    by_word = np.ascontiguousarray(scaled.reshape(k // 512, 128, 4, n).transpose(0, 1, 3, 2))
    if fmt == "e4m3":
        words = by_word.astype(ml_dtypes.float8_e4m3fn).view(np.uint8)
    else:
        c = by_word.astype(ml_dtypes.float4_e2m1fn).view(np.uint8) & 0xF
        words = c[..., 0::2] | (c[..., 1::2] << 4)
    return np.ascontiguousarray(words), np.ascontiguousarray(byte.astype(np.uint8).reshape(k // 512, 16, n))


def unpack_weight(words, scales, fmt):
    g, p, n, _ = words.shape
    if fmt == "e4m3":
        vals = np.ascontiguousarray(words).view(ml_dtypes.float8_e4m3fn).astype(np.float64)
    else:
        nib = np.empty((g, p, n, 4), np.uint8)
        nib[..., 0::2] = words & 0xF
        nib[..., 1::2] = words >> 4
        vals = E2M1[nib]
    vals = vals * np.repeat(np.exp2(scales.astype(np.float64) - 127.0), 8, axis=1)[..., None]
    return vals.transpose(0, 1, 3, 2).reshape(g * 512, n)


M, N, H = 128, 512, 8192
RMIN, RMAX = 0.4, 0.99
FMT = "e4m3"


def half_glorot(rows, cols):
    limit = np.sqrt(1.5 / ((rows + cols) / 2.0))
    return np.random.uniform(-limit, limit, (rows, cols))


def setup_inputs():
    s, t = mx_kscale(N), mx_kscale(H)
    inputs = np.random.standard_normal((M, N))
    state_re = np.random.standard_normal((M, H))
    state_im = np.random.standard_normal((M, H))
    C_re = half_glorot(H, N)
    C_im = half_glorot(H, N)
    B_re = half_glorot(N, H)
    B_im = half_glorot(N, H)
    D = np.random.standard_normal(N)
    nu = np.random.uniform(np.log(-np.log(RMAX)), np.log(-np.log(RMIN)), H)
    theta = np.random.uniform(0.0, 3.14 / 10, H)
    gamma = np.sqrt(1.0 - np.exp(-2.0 * np.exp(nu)))
    B_re_words, B_re_scales = pack_weight(B_re / s[:, None], FMT)
    B_im_words, B_im_scales = pack_weight(B_im / s[:, None], FMT)
    C_re_words, C_re_scales = pack_weight(C_re / t[:, None], FMT)
    C_im_words, C_im_scales = pack_weight(C_im / t[:, None], FMT)
    return {"inputs": bf(inputs * s), "state_re": bf(state_re * t), "state_im": bf(state_im * t),
            "B_re_words": B_re_words, "B_re_scales": B_re_scales,
            "B_im_words": B_im_words, "B_im_scales": B_im_scales,
            "C_re_words": C_re_words, "C_re_scales": C_re_scales,
            "C_im_words": C_im_words, "C_im_scales": C_im_scales,
            "D": bf(D / s), "nu": bf(nu), "theta": bf(theta), "gamma": bf(gamma * t)}


def reference(inputs, state_re, state_im, B_re_words, B_re_scales, B_im_words, B_im_scales,
              C_re_words, C_re_scales, C_im_words, C_im_scales, D, nu, theta, gamma):
    u = f64(inputs)
    mag = np.exp(-np.exp(f64(nu)))
    lam_re = mag * np.cos(f64(theta))
    lam_im = mag * np.sin(f64(theta))
    uq = mxq(u, 1, "e4m3")
    new_u_re = f64(gamma) * (uq @ unpack_weight(B_re_words, B_re_scales, FMT))
    new_u_im = f64(gamma) * (uq @ unpack_weight(B_im_words, B_im_scales, FMT))
    x_re = f64(state_re) * lam_re - f64(state_im) * lam_im + new_u_re
    x_im = f64(state_re) * lam_im + f64(state_im) * lam_re + new_u_im
    y = (mxq(x_re, 1, "e4m3") @ unpack_weight(C_re_words, C_re_scales, FMT)) - (mxq(x_im, 1, "e4m3") @ unpack_weight(C_im_words, C_im_scales, FMT)) + f64(D) * u
    return y, x_re, x_im

@@ -1,0 +1,382 @@
+import math
+from contextlib import ExitStack
+
+import concourse.mybir as mybir
+from concourse.masks import make_identity
+
+F32 = mybir.dt.float32
+BF16 = mybir.dt.bfloat16
+I32 = mybir.dt.int32
+U32 = mybir.dt.uint32
+U8 = mybir.dt.uint8
+FP8X4 = mybir.dt.float8_e4m3fn_x4
+ALU = mybir.AluOpType
+ACT = mybir.ActivationFunctionType
+
+P = 128
+N_IN = 512
+H = 8192
+UNIT = 512
+UNITS = H // UNIT
+BLOCK = P
+BLOCKS = UNIT // BLOCK
+ALL_BLOCKS = H // BLOCK
+PARTS = 2
+PACK = 4
+CHUNK_UNITS = 2
+CHUNK = CHUNK_UNITS * UNIT
+CHUNKS = UNITS // CHUNK_UNITS
+QUADRANTS = 4
+PLANES = 4
+
+FLOPS = 4 * 2 * P * N_IN * H
+
+TWO_PI_HI = 6.28125
+TWO_PI_MID = 2029.0 / 1048576.0
+TWO_PI_LO = 2.0 * math.pi - TWO_PI_HI - TWO_PI_MID
+ROUND_TO_INT = 12582912.0
+
+
+def tile_linearrecurrentunitcell_k_kernel(
+    tc,
+    inputs,
+    state_re,
+    state_im,
+    B_re_words,
+    B_re_scales,
+    B_im_words,
+    B_im_scales,
+    C_re_words,
+    C_re_scales,
+    C_im_words,
+    C_im_scales,
+    D,
+    nu,
+    theta,
+    gamma,
+    out_0,
+    out_1,
+    out_2,
+):
+    nc = tc.nc
+    state_in = (state_re, state_im)
+    b_words_in = (B_re_words, B_im_words)
+    b_scales_in = (B_re_scales, B_im_scales)
+    c_words_in = (C_re_words, C_im_words)
+    c_scales_in = (C_re_scales, C_im_scales)
+    new_out = (out_1, out_2)
+
+    with ExitStack() as stack:
+        stack.enter_context(tc.manual_schedule())
+        keep = stack.enter_context(tc.tile_pool(name="keep", bufs=1))
+        xt_pool = stack.enter_context(tc.tile_pool(name="xt", bufs=3))
+        work = stack.enter_context(tc.tile_pool(name="work", bufs=2))
+        st_psum = stack.enter_context(tc.psum_pool(name="st_psum", bufs=2))
+        pt_psum = stack.enter_context(tc.psum_pool(name="pt_psum", bufs=2))
+        xb_psum = stack.enter_context(tc.psum_pool(name="xb_psum", bufs=2))
+        xw_psum = stack.enter_context(tc.psum_pool(name="xw_psum", bufs=1))
+        y_psum = stack.enter_context(tc.psum_pool(name="y_psum", bufs=1))
+
+        b_planes = []
+        c_planes = []
+        for part in range(PARTS):
+            b_plane = keep.tile([P, H // PLANES], U8, name="b_plane%d" % part, align_bytes=64)
+            nc.vector.memset(b_plane[:].bitcast(I32), 0)
+            b_planes.append(b_plane)
+        for part in range(PARTS):
+            c_plane = keep.tile([P, UNITS // PLANES, N_IN], U8, name="c_plane%d" % part, align_bytes=64)
+            nc.vector.memset(c_plane[:].rearrange("p g n -> p (g n)").bitcast(I32), 0)
+            c_planes.append(c_plane)
+        par_b = keep.tile([P, P], BF16, name="par_b")
+        nc.vector.memset(par_b[:], 0.0)
+        d_row = keep.tile([P, N_IN], BF16, name="d_row")
+        nc.vector.memset(d_row[:], 0.0)
+        ones = keep.tile([P, P], BF16, name="ones")
+        nc.vector.memset(ones[:], 1.0)
+        ident_bf = keep.tile([P, P], BF16, name="ident_bf")
+        make_identity(nc, ident_bf[:])
+        ident_f32 = keep.tile([P, P], F32, name="ident_f32")
+        make_identity(nc, ident_f32[:])
+
+        par_a = keep.tile([P, P], BF16, name="par_a")
+        nc.scalar.dma_start(out=par_a[0:ALL_BLOCKS, :], in_=nu.rearrange("(j c) -> j c", c=BLOCK))
+        nc.scalar.dma_start(out=par_a[ALL_BLOCKS:P, :], in_=theta.rearrange("(j c) -> j c", c=BLOCK))
+        nc.scalar.dma_start(out=par_b[0:ALL_BLOCKS, :], in_=gamma.rearrange("(j c) -> j c", c=BLOCK))
+        u_sb = keep.tile([P, N_IN], BF16, name="u_sb")
+        nc.scalar.dma_start(out=u_sb[:], in_=inputs)
+        nc.scalar.dma_start(out=d_row[0:1, :], in_=D.rearrange("(o n) -> o n", o=1))
+
+        for part in range(PARTS):
+            for quad in range(QUADRANTS):
+                rows = b_scales_in[part][0, 4 * quad : 4 * quad + 4, :]
+                nc.sync.dma_start(
+                    out=b_planes[part][32 * quad : 32 * quad + 16, :].bitcast(I32),
+                    in_=rows.rearrange("r (k n) -> k r n", k=PLANES).bitcast(I32),
+                )
+        state_sb = []
+        b_words = []
+        c_words = []
+        for chunk in range(CHUNKS):
+            cols = slice(chunk * CHUNK, (chunk + 1) * CHUNK)
+            state_sb.append([])
+            b_words.append([])
+            c_words.append([])
+            for part in range(PARTS):
+                st = keep.tile([P, CHUNK], BF16, name="state%d_%d" % (part, chunk))
+                nc.sync.dma_start(out=st[:], in_=state_in[part][:, cols])
+                state_sb[chunk].append(st)
+            for part in range(PARTS):
+                bw = keep.tile([P, CHUNK], U32, name="b_words%d_%d" % (part, chunk), align_bytes=64)
+                flat = b_words_in[part][0].rearrange("p n t -> p (n t)")
+                nc.sync.dma_start(
+                    out=bw[:].bitcast(I32),
+                    in_=flat[:, 4 * chunk * CHUNK : 4 * (chunk + 1) * CHUNK].bitcast(I32),
+                )
+                b_words[chunk].append(bw)
+            if (chunk * CHUNK_UNITS) % PLANES == 0:
+                group = chunk * CHUNK_UNITS // PLANES
+                for part in range(PARTS):
+                    for quad in range(QUADRANTS):
+                        nc.sync.dma_start(
+                            out=c_planes[part][32 * quad : 32 * quad + 16, group, :].bitcast(I32),
+                            in_=c_scales_in[part][
+                                PLANES * group : PLANES * (group + 1), 4 * quad : 4 * quad + 4, :
+                            ].bitcast(I32),
+                        )
+            for part in range(PARTS):
+                cw = keep.tile([P, CHUNK_UNITS, N_IN], U32, name="c_words%d_%d" % (part, chunk), align_bytes=64)
+                passes = c_words_in[part][chunk * CHUNK_UNITS : (chunk + 1) * CHUNK_UNITS]
+                nc.sync.dma_start(
+                    out=cw[:].bitcast(I32),
+                    in_=passes.rearrange("g p n t -> p g (n t)").bitcast(I32),
+                )
+                c_words[chunk].append(cw)
+
+        par_ps = xb_psum.tile([P, 2, P], BF16, name="par_ps", tag="xb")
+        nc.tensor.transpose(par_ps[:, 0, :], par_a[:], ident_bf[:])
+        nc.tensor.transpose(par_ps[:, 1, :], par_b[:], ident_bf[:])
+        uw_ps = xw_psum.tile([P, 2, P], F32, name="uw_ps", tag="xw")
+        for u in range(2):
+            nc.tensor.transpose(uw_ps[:, u, :], u_sb[:].bitcast(F32)[:, u : N_IN // 2 : 2], ident_f32[:])
+        d_ps = xb_psum.tile([P, N_IN], F32, name="d_ps", tag="xb")
+        nc.tensor.matmul(out=d_ps[:], lhsT=ones[:], rhs=d_row[:], start=True, stop=True)
+
+        par = keep.tile([P, 2, P], F32, name="par")
+        nc.vector.tensor_copy(out=par[:], in_=par_ps[:])
+        nu_t = par[:, 0, 0:ALL_BLOCKS]
+        theta_t = par[:, 0, ALL_BLOCKS:P]
+        gamma_t = par[:, 1, 0:ALL_BLOCKS]
+
+        def small(name):
+            return keep.tile([P, ALL_BLOCKS], F32, name=name)
+
+        decay = small("decay")
+        nc.scalar.activation(out=decay[:], in_=nu_t, func=ACT.Exp)
+        mag = small("mag")
+        nc.scalar.activation(out=mag[:], in_=decay[:], func=ACT.Exp, scale=-1.0)
+        turns = small("turns")
+        nc.vector.tensor_scalar(
+            out=turns[:], in0=theta_t, scalar1=1.0 / (2.0 * math.pi), scalar2=ROUND_TO_INT, op0=ALU.mult, op1=ALU.add
+        )
+        nc.vector.tensor_scalar(out=turns[:], in0=turns[:], scalar1=ROUND_TO_INT, scalar2=None, op0=ALU.subtract)
+        angle = small("angle")
+        nc.vector.scalar_tensor_tensor(
+            out=angle[:], in0=turns[:], scalar=-TWO_PI_HI, in1=theta_t, op0=ALU.mult, op1=ALU.add
+        )
+        nc.vector.scalar_tensor_tensor(
+            out=angle[:], in0=turns[:], scalar=-TWO_PI_MID, in1=angle[:], op0=ALU.mult, op1=ALU.add
+        )
+        nc.vector.scalar_tensor_tensor(
+            out=angle[:], in0=turns[:], scalar=-TWO_PI_LO, in1=angle[:], op0=ALU.mult, op1=ALU.add
+        )
+        sin_t = small("sin_t")
+        nc.scalar.activation(out=sin_t[:], in_=angle[:], func=ACT.Sin)
+        sin_half = small("sin_half")
+        nc.scalar.activation(out=sin_half[:], in_=angle[:], func=ACT.Sin, scale=0.5)
+
+        u_grouped = keep.tile([P, PACK * P], BF16, name="u_grouped", align_bytes=64)
+        nc.vector.tensor_copy(
+            out=u_grouped[:].bitcast(F32).rearrange("p (m u) -> p m u", u=2),
+            in_=uw_ps[:].rearrange("p u m -> p m u"),
+        )
+        skip = keep.tile([P, N_IN], F32, name="skip")
+        nc.vector.tensor_tensor(out=skip[:], in0=d_ps[:], in1=u_sb[:], op=ALU.mult)
+        u_codes = keep.tile([P, P], U32, name="u_codes", align_bytes=64)
+        u_scales = keep.tile([P, P], U8, name="u_scales", align_bytes=64)
+        nc.vector.quantize_mx(out=u_codes[:].bitcast(FP8X4), scales=u_scales[:], in_=u_grouped[:])
+
+        cos_t = small("cos_t")
+        nc.vector.tensor_tensor(out=cos_t[:], in0=sin_half[:], in1=sin_half[:], op=ALU.mult)
+        nc.vector.tensor_scalar(out=cos_t[:], in0=cos_t[:], scalar1=-2.0, scalar2=1.0, op0=ALU.mult, op1=ALU.add)
+        lam_re = small("lam_re")
+        nc.vector.tensor_tensor(out=lam_re[:], in0=mag[:], in1=cos_t[:], op=ALU.mult)
+        lam_im = small("lam_im")
+        nc.vector.tensor_tensor(out=lam_im[:], in0=mag[:], in1=sin_t[:], op=ALU.mult)
+        neg_lam_im = small("neg_lam_im")
+        nc.vector.tensor_scalar(out=neg_lam_im[:], in0=lam_im[:], scalar1=-1.0, scalar2=None, op0=ALU.mult)
+
+        y_ps = y_psum.tile([P, N_IN], F32, name="y_ps")
+        st_of = {}
+        pt_of = {}
+        xt_of = {}
+        xb_of = {}
+        x_of = {}
+        xbf_of = {}
+        xw_of = {}
+        xq_of = {}
+
+        def transpose_state(g):
+            st_of[g] = st_psum.tile([P, BLOCKS, PARTS, P], BF16, name="st")
+            src = state_sb[g // CHUNK_UNITS]
+            first = (g % CHUNK_UNITS) * UNIT
+            for b in range(BLOCKS):
+                for part in range(PARTS):
+                    nc.tensor.transpose(
+                        st_of[g][:, b, part, :],
+                        src[part][:, first + b * BLOCK : first + (b + 1) * BLOCK],
+                        ident_bf[:],
+                    )
+
+        def first_matmul(g):
+            pt_of[g] = []
+            first = (g % CHUNK_UNITS) * UNIT
+            offset = 4 * (g * UNIT // (H // PLANES))
+            for half in range(2):
+                pt = pt_psum.tile([P, BLOCKS // 2, PARTS, P], F32, name="pt")
+                pt_of[g].append(pt)
+                for b in range(BLOCKS // 2):
+                    block = half * (BLOCKS // 2) + b
+                    cols = slice(first + block * BLOCK, first + (block + 1) * BLOCK)
+                    plane_first = (g * UNIT + block * BLOCK) % (H // PLANES)
+                    for part in range(PARTS):
+                        nc.tensor.matmul_mx(
+                            out=pt[:, b, part, :],
+                            lhsT=b_words[g // CHUNK_UNITS][part][:, cols].bitcast(FP8X4),
+                            lhsT_scale=b_planes[part][offset:P, plane_first : plane_first + BLOCK],
+                            rhs=u_codes[:].bitcast(FP8X4),
+                            rhs_scale=u_scales[:],
+                            start=True,
+                            stop=True,
+                        )
+
+        def scale_by_gamma(g):
+            xt_of[g] = xt_pool.tile([P, BLOCKS, PARTS, P], F32, name="xt")
+            for block in range(BLOCKS):
+                j = g * BLOCKS + block
+                nc.scalar.activation(
+                    out=xt_of[g][:, block, :, :],
+                    in_=pt_of[g][block // 2][:, block % 2, :, :],
+                    func=ACT.Copy,
+                    scale=gamma_t[:, j : j + 1],
+                )
+
+        def add_state_terms(g):
+            xt = xt_of[g]
+            st = st_of[g]
+            for block in range(BLOCKS):
+                j = g * BLOCKS + block
+                nc.vector.scalar_tensor_tensor(
+                    out=xt[:, block, 0, :], in0=st[:, block, 1, :], scalar=neg_lam_im[:, j : j + 1],
+                    in1=xt[:, block, 0, :], op0=ALU.mult, op1=ALU.add,
+                )
+                nc.vector.scalar_tensor_tensor(
+                    out=xt[:, block, 1, :], in0=st[:, block, 0, :], scalar=lam_im[:, j : j + 1],
+                    in1=xt[:, block, 1, :], op0=ALU.mult, op1=ALU.add,
+                )
+            for block in range(BLOCKS):
+                j = g * BLOCKS + block
+                nc.vector.scalar_tensor_tensor(
+                    out=xt[:, block, :, :], in0=st[:, block, :, :], scalar=lam_re[:, j : j + 1],
+                    in1=xt[:, block, :, :], op0=ALU.mult, op1=ALU.add,
+                )
+
+        def transpose_back(g):
+            xb_of[g] = []
+            for part in range(PARTS):
+                xb = xb_psum.tile([P, UNIT], F32, name="xb", tag="xb")
+                xb_of[g].append(xb)
+                for block in range(BLOCKS):
+                    nc.tensor.transpose(
+                        xb[:, block * BLOCK : (block + 1) * BLOCK], xt_of[g][:, block, part, :], ident_f32[:]
+                    )
+
+        def copy_out_and_store(g):
+            chunk = g // CHUNK_UNITS
+            cols = slice((g % CHUNK_UNITS) * UNIT, (g % CHUNK_UNITS + 1) * UNIT)
+            if g % CHUNK_UNITS == 0:
+                x_of[chunk] = [work.tile([P, CHUNK], F32, name="x%d" % part) for part in range(PARTS)]
+            for part in range(PARTS):
+                nc.scalar.copy(out=x_of[chunk][part][:, cols], in_=xb_of[g][part][:])
+            if g % CHUNK_UNITS == CHUNK_UNITS - 1:
+                for part in range(PARTS):
+                    nc.gpsimd.dma_start(
+                        out=new_out[part][:, chunk * CHUNK : (chunk + 1) * CHUNK], in_=x_of[chunk][part][:]
+                    )
+
+        def round_to_bf16(g):
+            chunk = g // CHUNK_UNITS
+            cols = slice((g % CHUNK_UNITS) * UNIT, (g % CHUNK_UNITS + 1) * UNIT)
+            xbf_of[g] = work.tile([P, PARTS, UNIT], BF16, name="xbf")
+            nc.vector.tensor_copy(out=xbf_of[g][:, 0, :], in_=x_of[chunk][0][:, cols])
+            nc.vector.tensor_scalar(
+                out=xbf_of[g][:, 1, :], in0=x_of[chunk][1][:, cols], scalar1=-1.0, scalar2=None, op0=ALU.mult
+            )
+
+        def transpose_words(g):
+            xw_of[g] = xw_psum.tile([P, PARTS, 2, P], F32, name="xw", tag="xw")
+            for part in range(PARTS):
+                words = xbf_of[g][:, part, :].bitcast(F32)
+                for u in range(2):
+                    nc.tensor.transpose(xw_of[g][:, part, u, :], words[:, u : UNIT // 2 : 2], ident_f32[:])
+
+        def quantise(g):
+            grouped = work.tile([P, PARTS * P * PACK], BF16, name="grouped", align_bytes=64)
+            nc.scalar.copy(
+                out=grouped[:].bitcast(F32).rearrange("p (a m u) -> p a m u", a=PARTS, u=2),
+                in_=xw_of[g][:].rearrange("p a u m -> p a m u"),
+            )
+            codes = work.tile([P, PARTS * P], U32, name="codes", align_bytes=64)
+            scales = work.tile([P, PARTS * P], U8, name="scales", align_bytes=64)
+            nc.vector.quantize_mx(out=codes[:].bitcast(FP8X4), scales=scales[:], in_=grouped[:])
+            xq_of[g] = (codes, scales)
+
+        def second_matmul(g):
+            codes, scales = xq_of[g]
+            offset = 4 * (g % PLANES)
+            for part in range(PARTS):
+                nc.tensor.matmul_mx(
+                    out=y_ps[:],
+                    lhsT=codes[:, part * P : (part + 1) * P].bitcast(FP8X4),
+                    lhsT_scale=scales[:, part * P : (part + 1) * P],
+                    rhs=c_words[g // CHUNK_UNITS][part][:, g % CHUNK_UNITS, :].bitcast(FP8X4),
+                    rhs_scale=c_planes[part][offset:P, g // PLANES, :],
+                    start=(g == 0 and part == 0),
+                    stop=(g == UNITS - 1 and part == PARTS - 1),
+                )
+
+        def live(g):
+            return 0 <= g < UNITS
+
+        for i in range(UNITS + 4):
+            if live(i):
+                transpose_state(i)
+            if live(i - 2):
+                transpose_back(i - 2)
+            if live(i - 3):
+                transpose_words(i - 3)
+            if live(i):
+                first_matmul(i)
+            if live(i - 4):
+                second_matmul(i - 4)
+            if live(i - 2):
+                copy_out_and_store(i - 2)
+                round_to_bf16(i - 2)
+            if live(i - 3):
+                quantise(i - 3)
+            if live(i):
+                scale_by_gamma(i)
+                add_state_terms(i)
+
+        y_sb = keep.tile([P, N_IN], F32, name="y_sb")
+        nc.vector.tensor_tensor(out=y_sb[:], in0=y_ps[:], in1=skip[:], op=ALU.add)
+        nc.sync.dma_start(out=out_0, in_=y_sb[:])

@@ -28,6 +28,8 @@ CHUNK = CHUNK_UNITS * UNIT
 CHUNKS = UNITS // CHUNK_UNITS
 QUADRANTS = 4
 PLANES = 4
+STEPS_TO_SECOND_MATMUL = 4
+C_LAG_CHUNKS = STEPS_TO_SECOND_MATMUL // CHUNK_UNITS
 
 FLOPS = 4 * 2 * P * N_IN * H
 
@@ -113,44 +115,52 @@ def tile_linearrecurrentunitcell_k_kernel(
                     out=b_planes[part][32 * quad : 32 * quad + 16, :].bitcast(I32),
                     in_=rows.rearrange("r (k n) -> k r n", k=PLANES).bitcast(I32),
                 )
-        state_sb = []
-        b_words = []
-        c_words = []
-        for chunk in range(CHUNKS):
-            cols = slice(chunk * CHUNK, (chunk + 1) * CHUNK)
-            state_sb.append([])
-            b_words.append([])
-            c_words.append([])
-            for part in range(PARTS):
-                st = keep.tile([P, CHUNK], BF16, name="state%d_%d" % (part, chunk))
-                nc.sync.dma_start(out=st[:], in_=state_in[part][:, cols])
-                state_sb[chunk].append(st)
-            for part in range(PARTS):
-                bw = keep.tile([P, CHUNK], U32, name="b_words%d_%d" % (part, chunk), align_bytes=64)
-                flat = b_words_in[part][0].rearrange("p n t -> p (n t)")
+        state_sb = {}
+        b_words = {}
+        c_words = {}
+        c_scale_dmas = []
+
+        def load_next_c_scale_rows():
+            n = len(c_scale_dmas)
+            if n < (UNITS // PLANES) * PARTS * QUADRANTS:
+                group, part, quad = n // (PARTS * QUADRANTS), (n // QUADRANTS) % PARTS, n % QUADRANTS
                 nc.sync.dma_start(
-                    out=bw[:].bitcast(I32),
-                    in_=flat[:, 4 * chunk * CHUNK : 4 * (chunk + 1) * CHUNK].bitcast(I32),
+                    out=c_planes[part][32 * quad : 32 * quad + 16, group, :].bitcast(I32),
+                    in_=c_scales_in[part][
+                        PLANES * group : PLANES * (group + 1), 4 * quad : 4 * quad + 4, :
+                    ].bitcast(I32),
                 )
-                b_words[chunk].append(bw)
-            if (chunk * CHUNK_UNITS) % PLANES == 0:
-                group = chunk * CHUNK_UNITS // PLANES
+                c_scale_dmas.append(n)
+
+        for k in range(CHUNKS + C_LAG_CHUNKS):
+            if k < CHUNKS:
                 for part in range(PARTS):
-                    for quad in range(QUADRANTS):
-                        nc.sync.dma_start(
-                            out=c_planes[part][32 * quad : 32 * quad + 16, group, :].bitcast(I32),
-                            in_=c_scales_in[part][
-                                PLANES * group : PLANES * (group + 1), 4 * quad : 4 * quad + 4, :
-                            ].bitcast(I32),
-                        )
-            for part in range(PARTS):
-                cw = keep.tile([P, CHUNK_UNITS, N_IN], U32, name="c_words%d_%d" % (part, chunk), align_bytes=64)
-                passes = c_words_in[part][chunk * CHUNK_UNITS : (chunk + 1) * CHUNK_UNITS]
-                nc.sync.dma_start(
-                    out=cw[:].bitcast(I32),
-                    in_=passes.rearrange("g p n t -> p g (n t)").bitcast(I32),
-                )
-                c_words[chunk].append(cw)
+                    st = keep.tile([P, CHUNK], BF16, name="state%d_%d" % (part, k))
+                    nc.sync.dma_start(out=st[:], in_=state_in[part][:, k * CHUNK : (k + 1) * CHUNK])
+                    state_sb[k, part] = st
+                    load_next_c_scale_rows()
+                for part in range(PARTS):
+                    bw = keep.tile([P, CHUNK], U32, name="b_words%d_%d" % (part, k), align_bytes=64)
+                    flat = b_words_in[part][0].rearrange("p n t -> p (n t)")
+                    nc.sync.dma_start(
+                        out=bw[:].bitcast(I32),
+                        in_=flat[:, PACK * k * CHUNK : PACK * (k + 1) * CHUNK].bitcast(I32),
+                    )
+                    b_words[k, part] = bw
+                    load_next_c_scale_rows()
+            if k >= C_LAG_CHUNKS:
+                chunk = k - C_LAG_CHUNKS
+                for part in range(PARTS):
+                    cw = keep.tile(
+                        [P, CHUNK_UNITS, N_IN], U32, name="c_words%d_%d" % (part, chunk), align_bytes=64
+                    )
+                    passes = c_words_in[part][chunk * CHUNK_UNITS : (chunk + 1) * CHUNK_UNITS]
+                    nc.sync.dma_start(
+                        out=cw[:].bitcast(I32),
+                        in_=passes.rearrange("g p n t -> p g (n t)").bitcast(I32),
+                    )
+                    c_words[chunk, part] = cw
+                    load_next_c_scale_rows()
 
         par_ps = xb_psum.tile([P, 2, P], BF16, name="par_ps", tag="xb")
         nc.tensor.transpose(par_ps[:, 0, :], par_a[:], ident_bf[:])
@@ -227,13 +237,12 @@ def tile_linearrecurrentunitcell_k_kernel(
 
         def transpose_state(g):
             st_of[g] = st_psum.tile([P, BLOCKS, PARTS, P], BF16, name="st")
-            src = state_sb[g // CHUNK_UNITS]
             first = (g % CHUNK_UNITS) * UNIT
             for b in range(BLOCKS):
                 for part in range(PARTS):
                     nc.tensor.transpose(
                         st_of[g][:, b, part, :],
-                        src[part][:, first + b * BLOCK : first + (b + 1) * BLOCK],
+                        state_sb[g // CHUNK_UNITS, part][:, first + b * BLOCK : first + (b + 1) * BLOCK],
                         ident_bf[:],
                     )
 
@@ -251,7 +260,7 @@ def tile_linearrecurrentunitcell_k_kernel(
                     for part in range(PARTS):
                         nc.tensor.matmul_mx(
                             out=pt[:, b, part, :],
-                            lhsT=b_words[g // CHUNK_UNITS][part][:, cols].bitcast(FP8X4),
+                            lhsT=b_words[g // CHUNK_UNITS, part][:, cols].bitcast(FP8X4),
                             lhsT_scale=b_planes[part][offset:P, plane_first : plane_first + BLOCK],
                             rhs=u_codes[:].bitcast(FP8X4),
                             rhs_scale=u_scales[:],
@@ -348,7 +357,7 @@ def tile_linearrecurrentunitcell_k_kernel(
                     out=y_ps[:],
                     lhsT=codes[:, part * P : (part + 1) * P].bitcast(FP8X4),
                     lhsT_scale=scales[:, part * P : (part + 1) * P],
-                    rhs=c_words[g // CHUNK_UNITS][part][:, g % CHUNK_UNITS, :].bitcast(FP8X4),
+                    rhs=c_words[g // CHUNK_UNITS, part][:, g % CHUNK_UNITS, :].bitcast(FP8X4),
                     rhs_scale=c_planes[part][offset:P, g // PLANES, :],
                     start=(g == 0 and part == 0),
                     stop=(g == UNITS - 1 and part == PARTS - 1),
@@ -357,7 +366,7 @@ def tile_linearrecurrentunitcell_k_kernel(
         def live(g):
             return 0 <= g < UNITS
 
-        for i in range(UNITS + 4):
+        for i in range(UNITS + STEPS_TO_SECOND_MATMUL):
             if live(i):
                 transpose_state(i)
             if live(i - 2):
@@ -366,8 +375,8 @@ def tile_linearrecurrentunitcell_k_kernel(
                 transpose_words(i - 3)
             if live(i):
                 first_matmul(i)
-            if live(i - 4):
-                second_matmul(i - 4)
+            if live(i - STEPS_TO_SECOND_MATMUL):
+                second_matmul(i - STEPS_TO_SECOND_MATMUL)
             if live(i - 2):
                 copy_out_and_store(i - 2)
                 round_to_bf16(i - 2)

@@ -28,8 +28,10 @@ CHUNK = CHUNK_UNITS * UNIT
 CHUNKS = UNITS // CHUNK_UNITS
 QUADRANTS = 4
 PLANES = 4
-STEPS_TO_SECOND_MATMUL = 4
+STEPS_TO_SECOND_MATMUL = 6
+STEPS_TO_QUANTISE = 3
 C_LAG_CHUNKS = STEPS_TO_SECOND_MATMUL // CHUNK_UNITS
+C_SCALES_FROM_CHUNK = 2
 
 FLOPS = 4 * 2 * P * N_IN * H
 
@@ -73,28 +75,27 @@ def tile_linearrecurrentunitcell_k_kernel(
         keep = stack.enter_context(tc.tile_pool(name="keep", bufs=1))
         xt_pool = stack.enter_context(tc.tile_pool(name="xt", bufs=3))
         work = stack.enter_context(tc.tile_pool(name="work", bufs=2))
+        xq_pool = stack.enter_context(tc.tile_pool(name="xq", bufs=STEPS_TO_SECOND_MATMUL - STEPS_TO_QUANTISE + 1))
         st_psum = stack.enter_context(tc.psum_pool(name="st_psum", bufs=2))
         pt_psum = stack.enter_context(tc.psum_pool(name="pt_psum", bufs=2))
         xb_psum = stack.enter_context(tc.psum_pool(name="xb_psum", bufs=2))
         xw_psum = stack.enter_context(tc.psum_pool(name="xw_psum", bufs=1))
         y_psum = stack.enter_context(tc.psum_pool(name="y_psum", bufs=1))
 
-        b_planes = []
-        c_planes = []
-        for part in range(PARTS):
-            b_plane = keep.tile([P, H // PLANES], U8, name="b_plane%d" % part, align_bytes=64)
-            nc.vector.memset(b_plane[:].bitcast(I32), 0)
-            b_planes.append(b_plane)
-        for part in range(PARTS):
-            c_plane = keep.tile([P, UNITS // PLANES, N_IN], U8, name="c_plane%d" % part, align_bytes=64)
-            nc.vector.memset(c_plane[:].rearrange("p g n -> p (g n)").bitcast(I32), 0)
-            c_planes.append(c_plane)
         par_b = keep.tile([P, P], BF16, name="par_b")
-        nc.vector.memset(par_b[:], 0.0)
+        nc.vector.memset(par_b[ALL_BLOCKS:P, :], 0.0)
+        b_planes = [keep.tile([P, H // PLANES], U8, name="b_plane%d" % part, align_bytes=64) for part in range(PARTS)]
+        for part in reversed(range(PARTS)):
+            nc.vector.memset(b_planes[part][:].bitcast(I32), 0)
         d_row = keep.tile([P, N_IN], BF16, name="d_row")
         nc.vector.memset(d_row[:], 0.0)
         ones = keep.tile([P, P], BF16, name="ones")
         nc.vector.memset(ones[:], 1.0)
+        c_planes = []
+        for part in range(PARTS):
+            c_plane = keep.tile([P, UNITS // PLANES, N_IN], U8, name="c_plane%d" % part, align_bytes=64)
+            nc.vector.memset(c_plane[:].rearrange("p g n -> p (g n)").bitcast(I32), 0)
+            c_planes.append(c_plane)
         ident_bf = keep.tile([P, P], BF16, name="ident_bf")
         make_identity(nc, ident_bf[:])
         ident_f32 = keep.tile([P, P], F32, name="ident_f32")
@@ -106,15 +107,17 @@ def tile_linearrecurrentunitcell_k_kernel(
         nc.scalar.dma_start(out=par_b[0:ALL_BLOCKS, :], in_=gamma.rearrange("(j c) -> j c", c=BLOCK))
         u_sb = keep.tile([P, N_IN], BF16, name="u_sb")
         nc.scalar.dma_start(out=u_sb[:], in_=inputs)
-        nc.scalar.dma_start(out=d_row[0:1, :], in_=D.rearrange("(o n) -> o n", o=1))
 
-        for part in range(PARTS):
+        def load_b_scale_rows(part, queue, view):
             for quad in range(QUADRANTS):
                 rows = b_scales_in[part][0, 4 * quad : 4 * quad + 4, :]
-                nc.sync.dma_start(
-                    out=b_planes[part][32 * quad : 32 * quad + 16, :].bitcast(I32),
-                    in_=rows.rearrange("r (k n) -> k r n", k=PLANES).bitcast(I32),
+                queue.dma_start(
+                    out=b_planes[part][32 * quad : 32 * quad + 16, :].bitcast(view),
+                    in_=rows.rearrange("r (k n) -> k r n", k=PLANES).bitcast(view),
                 )
+
+        load_b_scale_rows(1, nc.gpsimd, F32)
+
         state_sb = {}
         b_words = {}
         c_words = {}
@@ -138,7 +141,8 @@ def tile_linearrecurrentunitcell_k_kernel(
                     st = keep.tile([P, CHUNK], BF16, name="state%d_%d" % (part, k))
                     nc.sync.dma_start(out=st[:], in_=state_in[part][:, k * CHUNK : (k + 1) * CHUNK])
                     state_sb[k, part] = st
-                    load_next_c_scale_rows()
+                    if k >= C_SCALES_FROM_CHUNK:
+                        load_next_c_scale_rows()
                 for part in range(PARTS):
                     bw = keep.tile([P, CHUNK], U32, name="b_words%d_%d" % (part, k), align_bytes=64)
                     flat = b_words_in[part][0].rearrange("p n t -> p (n t)")
@@ -147,7 +151,12 @@ def tile_linearrecurrentunitcell_k_kernel(
                         in_=flat[:, PACK * k * CHUNK : PACK * (k + 1) * CHUNK].bitcast(I32),
                     )
                     b_words[k, part] = bw
-                    load_next_c_scale_rows()
+                    if k >= C_SCALES_FROM_CHUNK:
+                        load_next_c_scale_rows()
+            if k == 0:
+                load_b_scale_rows(0, nc.sync, I32)
+            if k == 1:
+                nc.sync.dma_start(out=d_row[0:1, :], in_=D.rearrange("(o n) -> o n", o=1))
             if k >= C_LAG_CHUNKS:
                 chunk = k - C_LAG_CHUNKS
                 for part in range(PARTS):
@@ -168,8 +177,6 @@ def tile_linearrecurrentunitcell_k_kernel(
         uw_ps = xw_psum.tile([P, 2, P], F32, name="uw_ps", tag="xw")
         for u in range(2):
             nc.tensor.transpose(uw_ps[:, u, :], u_sb[:].bitcast(F32)[:, u : N_IN // 2 : 2], ident_f32[:])
-        d_ps = xb_psum.tile([P, N_IN], F32, name="d_ps", tag="xb")
-        nc.tensor.matmul(out=d_ps[:], lhsT=ones[:], rhs=d_row[:], start=True, stop=True)
 
         par = keep.tile([P, 2, P], F32, name="par")
         nc.vector.tensor_copy(out=par[:], in_=par_ps[:])
@@ -209,8 +216,6 @@ def tile_linearrecurrentunitcell_k_kernel(
             out=u_grouped[:].bitcast(F32).rearrange("p (m u) -> p m u", u=2),
             in_=uw_ps[:].rearrange("p u m -> p m u"),
         )
-        skip = keep.tile([P, N_IN], F32, name="skip")
-        nc.vector.tensor_tensor(out=skip[:], in0=d_ps[:], in1=u_sb[:], op=ALU.mult)
         u_codes = keep.tile([P, P], U32, name="u_codes", align_bytes=64)
         u_scales = keep.tile([P, P], U8, name="u_scales", align_bytes=64)
         nc.vector.quantize_mx(out=u_codes[:].bitcast(FP8X4), scales=u_scales[:], in_=u_grouped[:])
@@ -344,10 +349,17 @@ def tile_linearrecurrentunitcell_k_kernel(
                 out=grouped[:].bitcast(F32).rearrange("p (a m u) -> p a m u", a=PARTS, u=2),
                 in_=xw_of[g][:].rearrange("p a u m -> p a m u"),
             )
-            codes = work.tile([P, PARTS * P], U32, name="codes", align_bytes=64)
-            scales = work.tile([P, PARTS * P], U8, name="scales", align_bytes=64)
+            codes = xq_pool.tile([P, PARTS * P], U32, name="codes", align_bytes=64)
+            scales = xq_pool.tile([P, PARTS * P], U8, name="scales", align_bytes=64)
             nc.vector.quantize_mx(out=codes[:].bitcast(FP8X4), scales=scales[:], in_=grouped[:])
             xq_of[g] = (codes, scales)
+
+        skip = keep.tile([P, N_IN], F32, name="skip")
+
+        def skip_term():
+            d_ps = xb_psum.tile([P, N_IN], F32, name="d_ps", tag="xb")
+            nc.tensor.matmul(out=d_ps[:], lhsT=ones[:], rhs=d_row[:], start=True, stop=True)
+            nc.vector.tensor_tensor(out=skip[:], in0=d_ps[:], in1=u_sb[:], op=ALU.mult)
 
         def second_matmul(g):
             codes, scales = xq_of[g]
@@ -371,8 +383,10 @@ def tile_linearrecurrentunitcell_k_kernel(
                 transpose_state(i)
             if live(i - 2):
                 transpose_back(i - 2)
-            if live(i - 3):
-                transpose_words(i - 3)
+            if live(i - STEPS_TO_QUANTISE):
+                transpose_words(i - STEPS_TO_QUANTISE)
+            if i == UNITS + STEPS_TO_QUANTISE:
+                skip_term()
             if live(i):
                 first_matmul(i)
             if live(i - STEPS_TO_SECOND_MATMUL):
@@ -380,8 +394,8 @@ def tile_linearrecurrentunitcell_k_kernel(
             if live(i - 2):
                 copy_out_and_store(i - 2)
                 round_to_bf16(i - 2)
-            if live(i - 3):
-                quantise(i - 3)
+            if live(i - STEPS_TO_QUANTISE):
+                quantise(i - STEPS_TO_QUANTISE)
             if live(i):
                 scale_by_gamma(i)
                 add_state_terms(i)

@@ -31,6 +31,7 @@ PLANES = 4
 STEPS_TO_SECOND_MATMUL = 6
 STEPS_TO_QUANTISE = 3
 C_LAG_CHUNKS = STEPS_TO_SECOND_MATMUL // CHUNK_UNITS
+X_BUFS = 2
 C_SCALES_FROM_CHUNK = 2
 
 FLOPS = 4 * 2 * P * N_IN * H
@@ -75,6 +76,7 @@ def tile_linearrecurrentunitcell_k_kernel(
         keep = stack.enter_context(tc.tile_pool(name="keep", bufs=1))
         xt_pool = stack.enter_context(tc.tile_pool(name="xt", bufs=3))
         work = stack.enter_context(tc.tile_pool(name="work", bufs=2))
+        x_pool = stack.enter_context(tc.tile_pool(name="x", bufs=X_BUFS))
         xq_pool = stack.enter_context(tc.tile_pool(name="xq", bufs=STEPS_TO_SECOND_MATMUL - STEPS_TO_QUANTISE + 1))
         st_psum = stack.enter_context(tc.psum_pool(name="st_psum", bufs=2))
         pt_psum = stack.enter_context(tc.psum_pool(name="pt_psum", bufs=2))
@@ -220,15 +222,15 @@ def tile_linearrecurrentunitcell_k_kernel(
         u_scales = keep.tile([P, P], U8, name="u_scales", align_bytes=64)
         nc.vector.quantize_mx(out=u_codes[:].bitcast(FP8X4), scales=u_scales[:], in_=u_grouped[:])
 
+        lam_im = small("lam_im")
+        nc.vector.tensor_tensor(out=lam_im[:], in0=mag[:], in1=sin_t[:], op=ALU.mult)
         cos_t = small("cos_t")
         nc.vector.tensor_tensor(out=cos_t[:], in0=sin_half[:], in1=sin_half[:], op=ALU.mult)
+        neg_lam_im = small("neg_lam_im")
+        nc.vector.tensor_scalar(out=neg_lam_im[:], in0=lam_im[:], scalar1=-1.0, scalar2=None, op0=ALU.mult)
         nc.vector.tensor_scalar(out=cos_t[:], in0=cos_t[:], scalar1=-2.0, scalar2=1.0, op0=ALU.mult, op1=ALU.add)
         lam_re = small("lam_re")
         nc.vector.tensor_tensor(out=lam_re[:], in0=mag[:], in1=cos_t[:], op=ALU.mult)
-        lam_im = small("lam_im")
-        nc.vector.tensor_tensor(out=lam_im[:], in0=mag[:], in1=sin_t[:], op=ALU.mult)
-        neg_lam_im = small("neg_lam_im")
-        nc.vector.tensor_scalar(out=neg_lam_im[:], in0=lam_im[:], scalar1=-1.0, scalar2=None, op0=ALU.mult)
 
         y_ps = y_psum.tile([P, N_IN], F32, name="y_ps")
         st_of = {}
@@ -318,30 +320,34 @@ def tile_linearrecurrentunitcell_k_kernel(
             chunk = g // CHUNK_UNITS
             cols = slice((g % CHUNK_UNITS) * UNIT, (g % CHUNK_UNITS + 1) * UNIT)
             if g % CHUNK_UNITS == 0:
-                x_of[chunk] = [work.tile([P, CHUNK], F32, name="x%d" % part) for part in range(PARTS)]
+                x_of[chunk] = [x_pool.tile([P, CHUNK], F32, name="x%d" % part) for part in range(PARTS)]
             for part in range(PARTS):
                 nc.scalar.copy(out=x_of[chunk][part][:, cols], in_=xb_of[g][part][:])
             if g % CHUNK_UNITS == CHUNK_UNITS - 1:
+                queue = nc.gpsimd if chunk < CHUNKS - X_BUFS else nc.sync
                 for part in range(PARTS):
-                    nc.gpsimd.dma_start(
+                    queue.dma_start(
                         out=new_out[part][:, chunk * CHUNK : (chunk + 1) * CHUNK], in_=x_of[chunk][part][:]
                     )
 
         def round_to_bf16(g):
             chunk = g // CHUNK_UNITS
             cols = slice((g % CHUNK_UNITS) * UNIT, (g % CHUNK_UNITS + 1) * UNIT)
-            xbf_of[g] = work.tile([P, PARTS, UNIT], BF16, name="xbf")
-            nc.vector.tensor_copy(out=xbf_of[g][:, 0, :], in_=x_of[chunk][0][:, cols])
+            xbf_of[g] = work.tile([P, PARTS, 2, UNIT // 2], BF16, name="xbf")
+            sorted_re, sorted_im = [
+                x_of[chunk][part][:, cols].rearrange("m (p u e) -> m u p e", u=2, e=2) for part in range(PARTS)
+            ]
+            nc.vector.tensor_copy(out=xbf_of[g][:, 0, :, :].rearrange("m u (p e) -> m u p e", e=2), in_=sorted_re)
             nc.vector.tensor_scalar(
-                out=xbf_of[g][:, 1, :], in0=x_of[chunk][1][:, cols], scalar1=-1.0, scalar2=None, op0=ALU.mult
+                out=xbf_of[g][:, 1, :, :].rearrange("m u (p e) -> m u p e", e=2),
+                in0=sorted_im, scalar1=-1.0, scalar2=None, op0=ALU.mult,
             )
 
         def transpose_words(g):
             xw_of[g] = xw_psum.tile([P, PARTS, 2, P], F32, name="xw", tag="xw")
             for part in range(PARTS):
-                words = xbf_of[g][:, part, :].bitcast(F32)
                 for u in range(2):
-                    nc.tensor.transpose(xw_of[g][:, part, u, :], words[:, u : UNIT // 2 : 2], ident_f32[:])
+                    nc.tensor.transpose(xw_of[g][:, part, u, :], xbf_of[g][:, part, u, :].bitcast(F32), ident_f32[:])
 
         def quantise(g):
             grouped = work.tile([P, PARTS * P * PACK], BF16, name="grouped", align_bytes=64)
@@ -402,4 +408,4 @@ def tile_linearrecurrentunitcell_k_kernel(
 
         y_sb = keep.tile([P, N_IN], F32, name="y_sb")
         nc.vector.tensor_tensor(out=y_sb[:], in0=y_ps[:], in1=skip[:], op=ALU.add)
-        nc.sync.dma_start(out=out_0, in_=y_sb[:])
+        nc.scalar.dma_start(out=out_0, in_=y_sb[:])

@@ -23,6 +23,7 @@ BLOCKS = UNIT // BLOCK
 ALL_BLOCKS = H // BLOCK
 PARTS = 2
 PACK = 4
+LOAD_UNITS = (2, 2, 4, 4, 4)
 CHUNK_UNITS = 2
 CHUNK = CHUNK_UNITS * UNIT
 CHUNKS = UNITS // CHUNK_UNITS
@@ -32,7 +33,7 @@ STEPS_TO_SECOND_MATMUL = 6
 STEPS_TO_QUANTISE = 3
 C_LAG_CHUNKS = STEPS_TO_SECOND_MATMUL // CHUNK_UNITS
 X_BUFS = 2
-C_SCALES_FROM_CHUNK = 2
+C_SCALES_FROM_LOAD = 2
 
 FLOPS = 4 * 2 * P * N_IN * H
 
@@ -137,24 +138,33 @@ def tile_linearrecurrentunitcell_k_kernel(
                 )
                 c_scale_dmas.append(n)
 
+        def load_state_and_b(load):
+            units = LOAD_UNITS[load]
+            first_unit = sum(LOAD_UNITS[:load])
+            first, width = first_unit * UNIT, units * UNIT
+            for part in range(PARTS):
+                st = keep.tile([P, width], BF16, name="state%d_%d" % (part, load))
+                nc.sync.dma_start(out=st[:], in_=state_in[part][:, first : first + width])
+                for n in range(units):
+                    state_sb[first_unit + n, part] = (st, n * UNIT)
+                if load >= C_SCALES_FROM_LOAD:
+                    load_next_c_scale_rows()
+            for part in range(PARTS):
+                bw = keep.tile([P, width], U32, name="b_words%d_%d" % (part, load), align_bytes=64)
+                flat = b_words_in[part][0].rearrange("p n t -> p (n t)")
+                nc.sync.dma_start(
+                    out=bw[:].bitcast(I32), in_=flat[:, PACK * first : PACK * (first + width)].bitcast(I32)
+                )
+                for n in range(units):
+                    b_words[first_unit + n, part] = (bw, n * UNIT)
+                if load >= C_SCALES_FROM_LOAD:
+                    load_next_c_scale_rows()
+
+        load = 0
         for k in range(CHUNKS + C_LAG_CHUNKS):
-            if k < CHUNKS:
-                for part in range(PARTS):
-                    st = keep.tile([P, CHUNK], BF16, name="state%d_%d" % (part, k))
-                    nc.sync.dma_start(out=st[:], in_=state_in[part][:, k * CHUNK : (k + 1) * CHUNK])
-                    state_sb[k, part] = st
-                    if k >= C_SCALES_FROM_CHUNK:
-                        load_next_c_scale_rows()
-                for part in range(PARTS):
-                    bw = keep.tile([P, CHUNK], U32, name="b_words%d_%d" % (part, k), align_bytes=64)
-                    flat = b_words_in[part][0].rearrange("p n t -> p (n t)")
-                    nc.sync.dma_start(
-                        out=bw[:].bitcast(I32),
-                        in_=flat[:, PACK * k * CHUNK : PACK * (k + 1) * CHUNK].bitcast(I32),
-                    )
-                    b_words[k, part] = bw
-                    if k >= C_SCALES_FROM_CHUNK:
-                        load_next_c_scale_rows()
+            if load < len(LOAD_UNITS) and k * CHUNK_UNITS == sum(LOAD_UNITS[:load]):
+                load_state_and_b(load)
+                load += 1
             if k == 0:
                 load_b_scale_rows(0, nc.sync, I32)
             if k == 1:
@@ -172,6 +182,8 @@ def tile_linearrecurrentunitcell_k_kernel(
                     )
                     c_words[chunk, part] = cw
                     load_next_c_scale_rows()
+                    if chunk >= CHUNKS // 2:
+                        load_next_c_scale_rows()
 
         par_ps = xb_psum.tile([P, 2, P], BF16, name="par_ps", tag="xb")
         nc.tensor.transpose(par_ps[:, 0, :], par_a[:], ident_bf[:])
@@ -244,30 +256,28 @@ def tile_linearrecurrentunitcell_k_kernel(
 
         def transpose_state(g):
             st_of[g] = st_psum.tile([P, BLOCKS, PARTS, P], BF16, name="st")
-            first = (g % CHUNK_UNITS) * UNIT
             for b in range(BLOCKS):
                 for part in range(PARTS):
+                    st, first = state_sb[g, part]
                     nc.tensor.transpose(
-                        st_of[g][:, b, part, :],
-                        state_sb[g // CHUNK_UNITS, part][:, first + b * BLOCK : first + (b + 1) * BLOCK],
-                        ident_bf[:],
+                        st_of[g][:, b, part, :], st[:, first + b * BLOCK : first + (b + 1) * BLOCK], ident_bf[:]
                     )
 
         def first_matmul(g):
             pt_of[g] = []
-            first = (g % CHUNK_UNITS) * UNIT
             offset = 4 * (g * UNIT // (H // PLANES))
             for half in range(2):
                 pt = pt_psum.tile([P, BLOCKS // 2, PARTS, P], F32, name="pt")
                 pt_of[g].append(pt)
                 for b in range(BLOCKS // 2):
                     block = half * (BLOCKS // 2) + b
-                    cols = slice(first + block * BLOCK, first + (block + 1) * BLOCK)
                     plane_first = (g * UNIT + block * BLOCK) % (H // PLANES)
                     for part in range(PARTS):
+                        bw, first = b_words[g, part]
+                        cols = slice(first + block * BLOCK, first + (block + 1) * BLOCK)
                         nc.tensor.matmul_mx(
                             out=pt[:, b, part, :],
-                            lhsT=b_words[g // CHUNK_UNITS, part][:, cols].bitcast(FP8X4),
+                            lhsT=bw[:, cols].bitcast(FP8X4),
                             lhsT_scale=b_planes[part][offset:P, plane_first : plane_first + BLOCK],
                             rhs=u_codes[:].bitcast(FP8X4),
                             rhs_scale=u_scales[:],

@@ -29,7 +29,7 @@ CHUNK = CHUNK_UNITS * UNIT
 CHUNKS = UNITS // CHUNK_UNITS
 QUADRANTS = 4
 PLANES = 4
-STEPS_TO_SECOND_MATMUL = 6
+STEPS_TO_SECOND_MATMUL = 10
 STEPS_TO_QUANTISE = 3
 C_LAG_CHUNKS = STEPS_TO_SECOND_MATMUL // CHUNK_UNITS
 X_BUFS = 2
@@ -259,9 +259,13 @@ def tile_linearrecurrentunitcell_k_kernel(
             for b in range(BLOCKS):
                 for part in range(PARTS):
                     st, first = state_sb[g, part]
-                    nc.tensor.transpose(
-                        st_of[g][:, b, part, :], st[:, first + b * BLOCK : first + (b + 1) * BLOCK], ident_bf[:]
-                    )
+                    cols = slice(first + b * BLOCK, first + (b + 1) * BLOCK)
+                    if part == 1 or b % 2 == 0:
+                        nc.tensor.matmul(
+                            out=st_of[g][:, b, part, :], lhsT=st[:, cols], rhs=ident_bf[:], start=True, stop=True
+                        )
+                    else:
+                        nc.tensor.transpose(st_of[g][:, b, part, :], st[:, cols], ident_bf[:])
 
         def first_matmul(g):
             pt_of[g] = []

@@ -30,6 +30,7 @@ CHUNKS = UNITS // CHUNK_UNITS
 QUADRANTS = 4
 PLANES = 4
 STEPS_TO_SECOND_MATMUL = 10
+STATE_TRANSPOSES = 2
 STEPS_TO_QUANTISE = 3
 C_LAG_CHUNKS = STEPS_TO_SECOND_MATMUL // CHUNK_UNITS
 X_BUFS = 2
@@ -254,18 +255,24 @@ def tile_linearrecurrentunitcell_k_kernel(
         xw_of = {}
         xq_of = {}
 
-        def transpose_state(g):
-            st_of[g] = st_psum.tile([P, BLOCKS, PARTS, P], BF16, name="st")
+        def state_block_is_transposed(b, part):
+            return part == 0 and b < STATE_TRANSPOSES
+
+        def transpose_state(g, transposes):
+            if transposes:
+                st_of[g] = st_psum.tile([P, BLOCKS, PARTS, P], BF16, name="st")
             for b in range(BLOCKS):
                 for part in range(PARTS):
                     st, first = state_sb[g, part]
                     cols = slice(first + b * BLOCK, first + (b + 1) * BLOCK)
-                    if part == 1 or b % 2 == 0:
+                    if state_block_is_transposed(b, part) != transposes:
+                        continue
+                    if transposes:
+                        nc.tensor.transpose(st_of[g][:, b, part, :], st[:, cols], ident_bf[:])
+                    else:
                         nc.tensor.matmul(
                             out=st_of[g][:, b, part, :], lhsT=st[:, cols], rhs=ident_bf[:], start=True, stop=True
                         )
-                    else:
-                        nc.tensor.transpose(st_of[g][:, b, part, :], st[:, cols], ident_bf[:])
 
         def first_matmul(g):
             pt_of[g] = []
@@ -400,7 +407,7 @@ def tile_linearrecurrentunitcell_k_kernel(
 
         for i in range(UNITS + STEPS_TO_SECOND_MATMUL):
             if live(i):
-                transpose_state(i)
+                transpose_state(i, transposes=True)
             if live(i - 2):
                 transpose_back(i - 2)
             if live(i - STEPS_TO_QUANTISE):
@@ -408,6 +415,7 @@ def tile_linearrecurrentunitcell_k_kernel(
             if i == UNITS + STEPS_TO_QUANTISE:
                 skip_term()
             if live(i):
+                transpose_state(i, transposes=False)
                 first_matmul(i)
             if live(i - STEPS_TO_SECOND_MATMUL):
                 second_matmul(i - STEPS_TO_SECOND_MATMUL)

@@ -29,12 +29,12 @@ CHUNK = CHUNK_UNITS * UNIT
 CHUNKS = UNITS // CHUNK_UNITS
 QUADRANTS = 4
 PLANES = 4
-STEPS_TO_SECOND_MATMUL = 10
+STEPS_TO_SECOND_MATMUL = 8
 STATE_TRANSPOSES = 2
 STEPS_TO_QUANTISE = 3
 C_LAG_CHUNKS = STEPS_TO_SECOND_MATMUL // CHUNK_UNITS
-X_BUFS = 2
-C_SCALES_FROM_LOAD = 2
+C_LOADS_BEFORE_STORES = 2
+X_BUFS = 4
 
 FLOPS = 4 * 2 * P * N_IN * H
 
@@ -111,6 +111,7 @@ def tile_linearrecurrentunitcell_k_kernel(
         nc.scalar.dma_start(out=par_b[0:ALL_BLOCKS, :], in_=gamma.rearrange("(j c) -> j c", c=BLOCK))
         u_sb = keep.tile([P, N_IN], BF16, name="u_sb")
         nc.scalar.dma_start(out=u_sb[:], in_=inputs)
+        nc.scalar.dma_start(out=d_row[0:1, :], in_=D.rearrange("(o n) -> o n", o=1))
 
         def load_b_scale_rows(part, queue, view):
             for quad in range(QUADRANTS):
@@ -148,8 +149,6 @@ def tile_linearrecurrentunitcell_k_kernel(
                 nc.sync.dma_start(out=st[:], in_=state_in[part][:, first : first + width])
                 for n in range(units):
                     state_sb[first_unit + n, part] = (st, n * UNIT)
-                if load >= C_SCALES_FROM_LOAD:
-                    load_next_c_scale_rows()
             for part in range(PARTS):
                 bw = keep.tile([P, width], U32, name="b_words%d_%d" % (part, load), align_bytes=64)
                 flat = b_words_in[part][0].rearrange("p n t -> p (n t)")
@@ -158,33 +157,26 @@ def tile_linearrecurrentunitcell_k_kernel(
                 )
                 for n in range(units):
                     b_words[first_unit + n, part] = (bw, n * UNIT)
-                if load >= C_SCALES_FROM_LOAD:
-                    load_next_c_scale_rows()
 
-        load = 0
-        for k in range(CHUNKS + C_LAG_CHUNKS):
-            if load < len(LOAD_UNITS) and k * CHUNK_UNITS == sum(LOAD_UNITS[:load]):
-                load_state_and_b(load)
-                load += 1
-            if k == 0:
-                load_b_scale_rows(0, nc.sync, I32)
-            if k == 1:
-                nc.sync.dma_start(out=d_row[0:1, :], in_=D.rearrange("(o n) -> o n", o=1))
-            if k >= C_LAG_CHUNKS:
-                chunk = k - C_LAG_CHUNKS
-                for part in range(PARTS):
-                    cw = keep.tile(
-                        [P, CHUNK_UNITS, N_IN], U32, name="c_words%d_%d" % (part, chunk), align_bytes=64
-                    )
-                    passes = c_words_in[part][chunk * CHUNK_UNITS : (chunk + 1) * CHUNK_UNITS]
-                    nc.sync.dma_start(
-                        out=cw[:].bitcast(I32),
-                        in_=passes.rearrange("g p n t -> p g (n t)").bitcast(I32),
-                    )
-                    c_words[chunk, part] = cw
-                    load_next_c_scale_rows()
-                    if chunk >= CHUNKS // 2:
-                        load_next_c_scale_rows()
+        def load_c(chunk):
+            for part in range(PARTS):
+                cw = keep.tile([P, CHUNK_UNITS, N_IN], U32, name="c_words%d_%d" % (part, chunk), align_bytes=64)
+                passes = c_words_in[part][chunk * CHUNK_UNITS : (chunk + 1) * CHUNK_UNITS]
+                nc.sync.dma_start(
+                    out=cw[:].bitcast(I32), in_=passes.rearrange("g p n t -> p g (n t)").bitcast(I32)
+                )
+                c_words[chunk, part] = cw
+                load_next_c_scale_rows()
+                load_next_c_scale_rows()
+
+        load_state_and_b(0)
+        load_b_scale_rows(0, nc.sync, I32)
+        load_state_and_b(1)
+        load_state_and_b(2)
+        load_state_and_b(3)
+        for chunk in range(C_LOADS_BEFORE_STORES):
+            load_c(chunk)
+        load_state_and_b(4)
 
         par_ps = xb_psum.tile([P, 2, P], BF16, name="par_ps", tag="xb")
         nc.tensor.transpose(par_ps[:, 0, :], par_a[:], ident_bf[:])
@@ -345,11 +337,12 @@ def tile_linearrecurrentunitcell_k_kernel(
             for part in range(PARTS):
                 nc.scalar.copy(out=x_of[chunk][part][:, cols], in_=xb_of[g][part][:])
             if g % CHUNK_UNITS == CHUNK_UNITS - 1:
-                queue = nc.gpsimd if chunk < CHUNKS - X_BUFS else nc.sync
                 for part in range(PARTS):
-                    queue.dma_start(
+                    nc.sync.dma_start(
                         out=new_out[part][:, chunk * CHUNK : (chunk + 1) * CHUNK], in_=x_of[chunk][part][:]
                     )
+                if chunk + C_LOADS_BEFORE_STORES < CHUNKS:
+                    load_c(chunk + C_LOADS_BEFORE_STORES)
 
         def round_to_bf16(g):
             chunk = g // CHUNK_UNITS
@@ -381,12 +374,12 @@ def tile_linearrecurrentunitcell_k_kernel(
             nc.vector.quantize_mx(out=codes[:].bitcast(FP8X4), scales=scales[:], in_=grouped[:])
             xq_of[g] = (codes, scales)
 
-        skip = keep.tile([P, N_IN], F32, name="skip")
+        y_sb = keep.tile([P, N_IN], F32, name="y_sb")
 
         def skip_term():
             d_ps = xb_psum.tile([P, N_IN], F32, name="d_ps", tag="xb")
             nc.tensor.matmul(out=d_ps[:], lhsT=ones[:], rhs=d_row[:], start=True, stop=True)
-            nc.vector.tensor_tensor(out=skip[:], in0=d_ps[:], in1=u_sb[:], op=ALU.mult)
+            nc.vector.tensor_tensor(out=y_sb[:], in0=d_ps[:], in1=u_sb[:], op=ALU.mult)
 
         def second_matmul(g):
             codes, scales = xq_of[g]
@@ -428,6 +421,5 @@ def tile_linearrecurrentunitcell_k_kernel(
                 scale_by_gamma(i)
                 add_state_terms(i)
 
-        y_sb = keep.tile([P, N_IN], F32, name="y_sb")
-        nc.vector.tensor_tensor(out=y_sb[:], in0=y_ps[:], in1=skip[:], op=ALU.add)
+        nc.vector.tensor_tensor(out=y_sb[:], in0=y_ps[:], in1=y_sb[:], op=ALU.add)
         nc.scalar.dma_start(out=out_0, in_=y_sb[:])

@@ -113,15 +113,14 @@ def tile_linearrecurrentunitcell_k_kernel(
         nc.scalar.dma_start(out=u_sb[:], in_=inputs)
         nc.scalar.dma_start(out=d_row[0:1, :], in_=D.rearrange("(o n) -> o n", o=1))
 
-        def load_b_scale_rows(part, queue, view):
+        def load_b_scale_rows(part):
             for quad in range(QUADRANTS):
                 rows = b_scales_in[part][0, 4 * quad : 4 * quad + 4, :]
-                queue.dma_start(
-                    out=b_planes[part][32 * quad : 32 * quad + 16, :].bitcast(view),
-                    in_=rows.rearrange("r (k n) -> k r n", k=PLANES).bitcast(view),
+                nc.sync.dma_start(
+                    out=b_planes[part][32 * quad : 32 * quad + 16, :].bitcast(I32),
+                    in_=rows.rearrange("r (k n) -> k r n", k=PLANES).bitcast(I32),
                 )
 
-        load_b_scale_rows(1, nc.gpsimd, F32)
 
         state_sb = {}
         b_words = {}
@@ -170,7 +169,8 @@ def tile_linearrecurrentunitcell_k_kernel(
                 load_next_c_scale_rows()
 
         load_state_and_b(0)
-        load_b_scale_rows(0, nc.sync, I32)
+        for part in range(PARTS):
+            load_b_scale_rows(part)
         load_state_and_b(1)
         load_state_and_b(2)
         load_state_and_b(3)

import math
from contextlib import ExitStack

import concourse.mybir as mybir
from concourse.masks import make_identity

F32 = mybir.dt.float32
BF16 = mybir.dt.bfloat16
I32 = mybir.dt.int32
U32 = mybir.dt.uint32
U8 = mybir.dt.uint8
FP8X4 = mybir.dt.float8_e4m3fn_x4
ALU = mybir.AluOpType
ACT = mybir.ActivationFunctionType

P = 128
N_IN = 512
H = 8192
UNIT = 512
UNITS = H // UNIT
BLOCK = P
BLOCKS = UNIT // BLOCK
ALL_BLOCKS = H // BLOCK
PARTS = 2
PACK = 4
LOAD_UNITS = (2, 2, 4, 4, 4)
CHUNK_UNITS = 2
CHUNK = CHUNK_UNITS * UNIT
CHUNKS = UNITS // CHUNK_UNITS
QUADRANTS = 4
PLANES = 4
STEPS_TO_SECOND_MATMUL = 8
STATE_TRANSPOSES = 2
STEPS_TO_QUANTISE = 3
C_LAG_CHUNKS = STEPS_TO_SECOND_MATMUL // CHUNK_UNITS
C_LOADS_BEFORE_STORES = 2
X_BUFS = 4

FLOPS = 4 * 2 * P * N_IN * H

TWO_PI_HI = 6.28125
TWO_PI_MID = 2029.0 / 1048576.0
TWO_PI_LO = 2.0 * math.pi - TWO_PI_HI - TWO_PI_MID
ROUND_TO_INT = 12582912.0


def tile_linearrecurrentunitcell_k_kernel(
    tc,
    inputs,
    state_re,
    state_im,
    B_re_words,
    B_re_scales,
    B_im_words,
    B_im_scales,
    C_re_words,
    C_re_scales,
    C_im_words,
    C_im_scales,
    D,
    nu,
    theta,
    gamma,
    out_0,
    out_1,
    out_2,
):
    nc = tc.nc
    state_in = (state_re, state_im)
    b_words_in = (B_re_words, B_im_words)
    b_scales_in = (B_re_scales, B_im_scales)
    c_words_in = (C_re_words, C_im_words)
    c_scales_in = (C_re_scales, C_im_scales)
    new_out = (out_1, out_2)

    with ExitStack() as stack:
        stack.enter_context(tc.manual_schedule())
        keep = stack.enter_context(tc.tile_pool(name="keep", bufs=1))
        xt_pool = stack.enter_context(tc.tile_pool(name="xt", bufs=3))
        work = stack.enter_context(tc.tile_pool(name="work", bufs=2))
        x_pool = stack.enter_context(tc.tile_pool(name="x", bufs=X_BUFS))
        xq_pool = stack.enter_context(tc.tile_pool(name="xq", bufs=STEPS_TO_SECOND_MATMUL - STEPS_TO_QUANTISE + 1))
        st_psum = stack.enter_context(tc.psum_pool(name="st_psum", bufs=2))
        pt_psum = stack.enter_context(tc.psum_pool(name="pt_psum", bufs=2))
        xb_psum = stack.enter_context(tc.psum_pool(name="xb_psum", bufs=2))
        xw_psum = stack.enter_context(tc.psum_pool(name="xw_psum", bufs=1))
        y_psum = stack.enter_context(tc.psum_pool(name="y_psum", bufs=1))

        par_b = keep.tile([P, P], BF16, name="par_b")
        nc.vector.memset(par_b[ALL_BLOCKS:P, :], 0.0)
        b_planes = [keep.tile([P, H // PLANES], U8, name="b_plane%d" % part, align_bytes=64) for part in range(PARTS)]
        for part in reversed(range(PARTS)):
            nc.vector.memset(b_planes[part][:].bitcast(I32), 0)
        d_row = keep.tile([P, N_IN], BF16, name="d_row")
        nc.vector.memset(d_row[:], 0.0)
        ones = keep.tile([P, P], BF16, name="ones")
        nc.vector.memset(ones[:], 1.0)
        c_planes = []
        for part in range(PARTS):
            c_plane = keep.tile([P, UNITS // PLANES, N_IN], U8, name="c_plane%d" % part, align_bytes=64)
            nc.vector.memset(c_plane[:].rearrange("p g n -> p (g n)").bitcast(I32), 0)
            c_planes.append(c_plane)
        ident_bf = keep.tile([P, P], BF16, name="ident_bf")
        make_identity(nc, ident_bf[:])
        ident_f32 = keep.tile([P, P], F32, name="ident_f32")
        make_identity(nc, ident_f32[:])

        par_a = keep.tile([P, P], BF16, name="par_a")
        nc.scalar.dma_start(out=par_a[0:ALL_BLOCKS, :], in_=nu.rearrange("(j c) -> j c", c=BLOCK))
        nc.scalar.dma_start(out=par_a[ALL_BLOCKS:P, :], in_=theta.rearrange("(j c) -> j c", c=BLOCK))
        nc.scalar.dma_start(out=par_b[0:ALL_BLOCKS, :], in_=gamma.rearrange("(j c) -> j c", c=BLOCK))
        u_sb = keep.tile([P, N_IN], BF16, name="u_sb")
        nc.scalar.dma_start(out=u_sb[:], in_=inputs)
        nc.scalar.dma_start(out=d_row[0:1, :], in_=D.rearrange("(o n) -> o n", o=1))

        def load_b_scale_rows(part):
            for quad in range(QUADRANTS):
                rows = b_scales_in[part][0, 4 * quad : 4 * quad + 4, :]
                nc.sync.dma_start(
                    out=b_planes[part][32 * quad : 32 * quad + 16, :].bitcast(I32),
                    in_=rows.rearrange("r (k n) -> k r n", k=PLANES).bitcast(I32),
                )


        state_sb = {}
        b_words = {}
        c_words = {}
        c_scale_dmas = []

        def load_next_c_scale_rows():
            n = len(c_scale_dmas)
            if n < (UNITS // PLANES) * PARTS * QUADRANTS:
                group, part, quad = n // (PARTS * QUADRANTS), (n // QUADRANTS) % PARTS, n % QUADRANTS
                nc.sync.dma_start(
                    out=c_planes[part][32 * quad : 32 * quad + 16, group, :].bitcast(I32),
                    in_=c_scales_in[part][
                        PLANES * group : PLANES * (group + 1), 4 * quad : 4 * quad + 4, :
                    ].bitcast(I32),
                )
                c_scale_dmas.append(n)

        def load_state_and_b(load):
            units = LOAD_UNITS[load]
            first_unit = sum(LOAD_UNITS[:load])
            first, width = first_unit * UNIT, units * UNIT
            for part in range(PARTS):
                st = keep.tile([P, width], BF16, name="state%d_%d" % (part, load))
                nc.sync.dma_start(out=st[:], in_=state_in[part][:, first : first + width])
                for n in range(units):
                    state_sb[first_unit + n, part] = (st, n * UNIT)
            for part in range(PARTS):
                bw = keep.tile([P, width], U32, name="b_words%d_%d" % (part, load), align_bytes=64)
                flat = b_words_in[part][0].rearrange("p n t -> p (n t)")
                nc.sync.dma_start(
                    out=bw[:].bitcast(I32), in_=flat[:, PACK * first : PACK * (first + width)].bitcast(I32)
                )
                for n in range(units):
                    b_words[first_unit + n, part] = (bw, n * UNIT)

        def load_c(chunk):
            for part in range(PARTS):
                cw = keep.tile([P, CHUNK_UNITS, N_IN], U32, name="c_words%d_%d" % (part, chunk), align_bytes=64)
                passes = c_words_in[part][chunk * CHUNK_UNITS : (chunk + 1) * CHUNK_UNITS]
                nc.sync.dma_start(
                    out=cw[:].bitcast(I32), in_=passes.rearrange("g p n t -> p g (n t)").bitcast(I32)
                )
                c_words[chunk, part] = cw
                load_next_c_scale_rows()
                load_next_c_scale_rows()

        load_state_and_b(0)
        for part in range(PARTS):
            load_b_scale_rows(part)
        load_state_and_b(1)
        load_state_and_b(2)
        load_state_and_b(3)
        for chunk in range(C_LOADS_BEFORE_STORES):
            load_c(chunk)
        load_state_and_b(4)

        par_ps = xb_psum.tile([P, 2, P], BF16, name="par_ps", tag="xb")
        nc.tensor.transpose(par_ps[:, 0, :], par_a[:], ident_bf[:])
        nc.tensor.transpose(par_ps[:, 1, :], par_b[:], ident_bf[:])
        uw_ps = xw_psum.tile([P, 2, P], F32, name="uw_ps", tag="xw")
        for u in range(2):
            nc.tensor.transpose(uw_ps[:, u, :], u_sb[:].bitcast(F32)[:, u : N_IN // 2 : 2], ident_f32[:])

        par = keep.tile([P, 2, P], F32, name="par")
        nc.vector.tensor_copy(out=par[:], in_=par_ps[:])
        nu_t = par[:, 0, 0:ALL_BLOCKS]
        theta_t = par[:, 0, ALL_BLOCKS:P]
        gamma_t = par[:, 1, 0:ALL_BLOCKS]

        def small(name):
            return keep.tile([P, ALL_BLOCKS], F32, name=name)

        decay = small("decay")
        nc.scalar.activation(out=decay[:], in_=nu_t, func=ACT.Exp)
        mag = small("mag")
        nc.scalar.activation(out=mag[:], in_=decay[:], func=ACT.Exp, scale=-1.0)
        turns = small("turns")
        nc.vector.tensor_scalar(
            out=turns[:], in0=theta_t, scalar1=1.0 / (2.0 * math.pi), scalar2=ROUND_TO_INT, op0=ALU.mult, op1=ALU.add
        )
        nc.vector.tensor_scalar(out=turns[:], in0=turns[:], scalar1=ROUND_TO_INT, scalar2=None, op0=ALU.subtract)
        angle = small("angle")
        nc.vector.scalar_tensor_tensor(
            out=angle[:], in0=turns[:], scalar=-TWO_PI_HI, in1=theta_t, op0=ALU.mult, op1=ALU.add
        )
        nc.vector.scalar_tensor_tensor(
            out=angle[:], in0=turns[:], scalar=-TWO_PI_MID, in1=angle[:], op0=ALU.mult, op1=ALU.add
        )
        nc.vector.scalar_tensor_tensor(
            out=angle[:], in0=turns[:], scalar=-TWO_PI_LO, in1=angle[:], op0=ALU.mult, op1=ALU.add
        )
        sin_t = small("sin_t")
        nc.scalar.activation(out=sin_t[:], in_=angle[:], func=ACT.Sin)
        sin_half = small("sin_half")
        nc.scalar.activation(out=sin_half[:], in_=angle[:], func=ACT.Sin, scale=0.5)

        u_grouped = keep.tile([P, PACK * P], BF16, name="u_grouped", align_bytes=64)
        nc.vector.tensor_copy(
            out=u_grouped[:].bitcast(F32).rearrange("p (m u) -> p m u", u=2),
            in_=uw_ps[:].rearrange("p u m -> p m u"),
        )
        u_codes = keep.tile([P, P], U32, name="u_codes", align_bytes=64)
        u_scales = keep.tile([P, P], U8, name="u_scales", align_bytes=64)
        nc.vector.quantize_mx(out=u_codes[:].bitcast(FP8X4), scales=u_scales[:], in_=u_grouped[:])

        lam_im = small("lam_im")
        nc.vector.tensor_tensor(out=lam_im[:], in0=mag[:], in1=sin_t[:], op=ALU.mult)
        cos_t = small("cos_t")
        nc.vector.tensor_tensor(out=cos_t[:], in0=sin_half[:], in1=sin_half[:], op=ALU.mult)
        neg_lam_im = small("neg_lam_im")
        nc.vector.tensor_scalar(out=neg_lam_im[:], in0=lam_im[:], scalar1=-1.0, scalar2=None, op0=ALU.mult)
        nc.vector.tensor_scalar(out=cos_t[:], in0=cos_t[:], scalar1=-2.0, scalar2=1.0, op0=ALU.mult, op1=ALU.add)
        lam_re = small("lam_re")
        nc.vector.tensor_tensor(out=lam_re[:], in0=mag[:], in1=cos_t[:], op=ALU.mult)

        y_ps = y_psum.tile([P, N_IN], F32, name="y_ps")
        st_of = {}
        pt_of = {}
        xt_of = {}
        xb_of = {}
        x_of = {}
        xbf_of = {}
        xw_of = {}
        xq_of = {}

        def state_block_is_transposed(b, part):
            return part == 0 and b < STATE_TRANSPOSES

        def transpose_state(g, transposes):
            if transposes:
                st_of[g] = st_psum.tile([P, BLOCKS, PARTS, P], BF16, name="st")
            for b in range(BLOCKS):
                for part in range(PARTS):
                    st, first = state_sb[g, part]
                    cols = slice(first + b * BLOCK, first + (b + 1) * BLOCK)
                    if state_block_is_transposed(b, part) != transposes:
                        continue
                    if transposes:
                        nc.tensor.transpose(st_of[g][:, b, part, :], st[:, cols], ident_bf[:])
                    else:
                        nc.tensor.matmul(
                            out=st_of[g][:, b, part, :], lhsT=st[:, cols], rhs=ident_bf[:], start=True, stop=True
                        )

        def first_matmul(g):
            pt_of[g] = []
            offset = 4 * (g * UNIT // (H // PLANES))
            for half in range(2):
                pt = pt_psum.tile([P, BLOCKS // 2, PARTS, P], F32, name="pt")
                pt_of[g].append(pt)
                for b in range(BLOCKS // 2):
                    block = half * (BLOCKS // 2) + b
                    plane_first = (g * UNIT + block * BLOCK) % (H // PLANES)
                    for part in range(PARTS):
                        bw, first = b_words[g, part]
                        cols = slice(first + block * BLOCK, first + (block + 1) * BLOCK)
                        nc.tensor.matmul_mx(
                            out=pt[:, b, part, :],
                            lhsT=bw[:, cols].bitcast(FP8X4),
                            lhsT_scale=b_planes[part][offset:P, plane_first : plane_first + BLOCK],
                            rhs=u_codes[:].bitcast(FP8X4),
                            rhs_scale=u_scales[:],
                            start=True,
                            stop=True,
                        )

        def scale_by_gamma(g):
            xt_of[g] = xt_pool.tile([P, BLOCKS, PARTS, P], F32, name="xt")
            for block in range(BLOCKS):
                j = g * BLOCKS + block
                nc.scalar.activation(
                    out=xt_of[g][:, block, :, :],
                    in_=pt_of[g][block // 2][:, block % 2, :, :],
                    func=ACT.Copy,
                    scale=gamma_t[:, j : j + 1],
                )

        def add_state_terms(g):
            xt = xt_of[g]
            st = st_of[g]
            for block in range(BLOCKS):
                j = g * BLOCKS + block
                nc.vector.scalar_tensor_tensor(
                    out=xt[:, block, 0, :], in0=st[:, block, 1, :], scalar=neg_lam_im[:, j : j + 1],
                    in1=xt[:, block, 0, :], op0=ALU.mult, op1=ALU.add,
                )
                nc.vector.scalar_tensor_tensor(
                    out=xt[:, block, 1, :], in0=st[:, block, 0, :], scalar=lam_im[:, j : j + 1],
                    in1=xt[:, block, 1, :], op0=ALU.mult, op1=ALU.add,
                )
            for block in range(BLOCKS):
                j = g * BLOCKS + block
                nc.vector.scalar_tensor_tensor(
                    out=xt[:, block, :, :], in0=st[:, block, :, :], scalar=lam_re[:, j : j + 1],
                    in1=xt[:, block, :, :], op0=ALU.mult, op1=ALU.add,
                )

        def transpose_back(g):
            xb_of[g] = []
            for part in range(PARTS):
                xb = xb_psum.tile([P, UNIT], F32, name="xb", tag="xb")
                xb_of[g].append(xb)
                for block in range(BLOCKS):
                    nc.tensor.transpose(
                        xb[:, block * BLOCK : (block + 1) * BLOCK], xt_of[g][:, block, part, :], ident_f32[:]
                    )

        def copy_out_and_store(g):
            chunk = g // CHUNK_UNITS
            cols = slice((g % CHUNK_UNITS) * UNIT, (g % CHUNK_UNITS + 1) * UNIT)
            if g % CHUNK_UNITS == 0:
                x_of[chunk] = [x_pool.tile([P, CHUNK], F32, name="x%d" % part) for part in range(PARTS)]
            for part in range(PARTS):
                nc.scalar.copy(out=x_of[chunk][part][:, cols], in_=xb_of[g][part][:])
            if g % CHUNK_UNITS == CHUNK_UNITS - 1:
                for part in range(PARTS):
                    nc.sync.dma_start(
                        out=new_out[part][:, chunk * CHUNK : (chunk + 1) * CHUNK], in_=x_of[chunk][part][:]
                    )
                if chunk + C_LOADS_BEFORE_STORES < CHUNKS:
                    load_c(chunk + C_LOADS_BEFORE_STORES)

        def round_to_bf16(g):
            chunk = g // CHUNK_UNITS
            cols = slice((g % CHUNK_UNITS) * UNIT, (g % CHUNK_UNITS + 1) * UNIT)
            xbf_of[g] = work.tile([P, PARTS, 2, UNIT // 2], BF16, name="xbf")
            sorted_re, sorted_im = [
                x_of[chunk][part][:, cols].rearrange("m (p u e) -> m u p e", u=2, e=2) for part in range(PARTS)
            ]
            nc.vector.tensor_copy(out=xbf_of[g][:, 0, :, :].rearrange("m u (p e) -> m u p e", e=2), in_=sorted_re)
            nc.vector.tensor_scalar(
                out=xbf_of[g][:, 1, :, :].rearrange("m u (p e) -> m u p e", e=2),
                in0=sorted_im, scalar1=-1.0, scalar2=None, op0=ALU.mult,
            )

        def transpose_words(g):
            xw_of[g] = xw_psum.tile([P, PARTS, 2, P], F32, name="xw", tag="xw")
            for part in range(PARTS):
                for u in range(2):
                    nc.tensor.transpose(xw_of[g][:, part, u, :], xbf_of[g][:, part, u, :].bitcast(F32), ident_f32[:])

        def quantise(g):
            grouped = work.tile([P, PARTS * P * PACK], BF16, name="grouped", align_bytes=64)
            nc.scalar.copy(
                out=grouped[:].bitcast(F32).rearrange("p (a m u) -> p a m u", a=PARTS, u=2),
                in_=xw_of[g][:].rearrange("p a u m -> p a m u"),
            )
            codes = xq_pool.tile([P, PARTS * P], U32, name="codes", align_bytes=64)
            scales = xq_pool.tile([P, PARTS * P], U8, name="scales", align_bytes=64)
            nc.vector.quantize_mx(out=codes[:].bitcast(FP8X4), scales=scales[:], in_=grouped[:])
            xq_of[g] = (codes, scales)

        y_sb = keep.tile([P, N_IN], F32, name="y_sb")

        def skip_term():
            d_ps = xb_psum.tile([P, N_IN], F32, name="d_ps", tag="xb")
            nc.tensor.matmul(out=d_ps[:], lhsT=ones[:], rhs=d_row[:], start=True, stop=True)
            nc.vector.tensor_tensor(out=y_sb[:], in0=d_ps[:], in1=u_sb[:], op=ALU.mult)

        def second_matmul(g):
            codes, scales = xq_of[g]
            offset = 4 * (g % PLANES)
            for part in range(PARTS):
                nc.tensor.matmul_mx(
                    out=y_ps[:],
                    lhsT=codes[:, part * P : (part + 1) * P].bitcast(FP8X4),
                    lhsT_scale=scales[:, part * P : (part + 1) * P],
                    rhs=c_words[g // CHUNK_UNITS, part][:, g % CHUNK_UNITS, :].bitcast(FP8X4),
                    rhs_scale=c_planes[part][offset:P, g // PLANES, :],
                    start=(g == 0 and part == 0),
                    stop=(g == UNITS - 1 and part == PARTS - 1),
                )

        def live(g):
            return 0 <= g < UNITS

        for i in range(UNITS + STEPS_TO_SECOND_MATMUL):
            if live(i):
                transpose_state(i, transposes=True)
            if live(i - 2):
                transpose_back(i - 2)
            if live(i - STEPS_TO_QUANTISE):
                transpose_words(i - STEPS_TO_QUANTISE)
            if i == UNITS + STEPS_TO_QUANTISE:
                skip_term()
            if live(i):
                transpose_state(i, transposes=False)
                first_matmul(i)
            if live(i - STEPS_TO_SECOND_MATMUL):
                second_matmul(i - STEPS_TO_SECOND_MATMUL)
            if live(i - 2):
                copy_out_and_store(i - 2)
                round_to_bf16(i - 2)
            if live(i - STEPS_TO_QUANTISE):
                quantise(i - STEPS_TO_QUANTISE)
            if live(i):
                scale_by_gamma(i)
                add_state_terms(i)

        nc.vector.tensor_tensor(out=y_sb[:], in0=y_ps[:], in1=y_sb[:], op=ALU.add)
        nc.scalar.dma_start(out=out_0, in_=y_sb[:])
